import numpy as np
import ml_dtypes


def mxq(x, axis, fmt="e4m3"):
    dtype, down = {"e4m3": (ml_dtypes.float8_e4m3fn, 7), "e5m2": (ml_dtypes.float8_e5m2, 14)}[fmt]
    v = np.moveaxis(np.asarray(x, np.float32).astype(ml_dtypes.bfloat16).astype(np.float64), axis, -1)
    blocks = v.reshape(v.shape[:-1] + (-1, 32))
    amax = np.abs(blocks).max(-1, keepdims=True)
    byte = np.maximum(np.where(amax > 0, np.frexp(amax)[1] - 1 + 127, 0) - down, 1)
    scale = np.exp2(byte - 127.0)
    codes = (blocks / scale).astype(np.float32).astype(dtype).astype(np.float64)
    return np.moveaxis((codes * scale).reshape(v.shape), -1, axis)


WIDE = False


def mx_kscale(k):
    if not WIDE:
        return np.ones(k)
    levels = np.array([10, -10, 5, -5, 0])
    if k % 512:
        return np.exp2(np.random.permutation(np.resize(levels, k // 32))).repeat(32)
    a = np.empty((k // 512, 16))
    for p in range(k // 512):
        a[p, :8] = np.random.permutation(np.resize(levels, 8))
        for g in range(8):
            far = levels[np.abs(levels - a[p, g]) >= 10]
            a[p, g + 8] = far[np.random.randint(len(far))]
    return np.exp2(a.ravel()).repeat(32)


BF16 = ml_dtypes.bfloat16


def bf(x):
    return np.asarray(x, np.float32).astype(BF16)


def f64(x):
    return np.asarray(x).astype(np.float64)


M, K, N = 8192, 1024, 128


def softplus(v):
    return np.logaddexp(v, 0.0)


def setup_inputs():
    s = mx_kscale(K)
    w_std0 = np.log(np.expm1(0.5 / np.sqrt(K)))
    return {"x": bf(np.random.standard_normal((M, K)) * s),
            "w_loc": bf(np.random.standard_normal((K, N)) * 0.9 / np.sqrt(K) / s[:, None]),
            "w_std": bf(w_std0 + 0.3 * np.random.standard_normal((K, N))),
            "b_loc": bf(np.random.standard_normal((1, N)) * 0.5),
            "b_std": bf(-1.0 + 0.3 * np.random.standard_normal((1, N))),
            "eps_w": bf(np.random.standard_normal((K, N)) / s[:, None]),
            "eps_b": bf(np.random.standard_normal((1, N)))}


def reference(x, w_loc, w_std, b_loc, b_std, eps_w, eps_b):
    w = f64(w_loc) + softplus(f64(w_std)) * f64(eps_w)
    b = f64(b_loc) + softplus(f64(b_std)) * f64(eps_b)
    return (mxq(f64(x), 1, "e4m3") @ mxq(w, 0, "e4m3")) + b

@@ -1,0 +1,230 @@
+from contextlib import ExitStack
+
+import concourse.mybir as mybir
+from concourse.masks import make_identity
+
+F32 = mybir.dt.float32
+BF16 = mybir.dt.bfloat16
+U32 = mybir.dt.uint32
+U8 = mybir.dt.uint8
+FP8X4 = mybir.dt.float8_e4m3fn_x4
+ALU = mybir.AluOpType
+ACT = mybir.ActivationFunctionType
+
+P = 128
+ROWS, K, N = 8192, 1024, 128
+FLOPS = 2 * ROWS * K * N
+J = ROWS // P
+JC = 4
+NCH = J // JC
+CH = JC * K
+STORES = [(0, 32), (32, 48), (48, 56), (56, 60), (60, 62), (62, 64)]
+M_LAG = 3
+O_LAG = 4
+
+
+def dve_banks(c):
+    if c == 0:
+        return (0, 1, 2)
+    if c in (6, 11):
+        return (0,)
+    return ()
+
+
+def tile_bayesiandenselayer_t_kernel(tc, x, w_loc, w_std, b_loc, b_std, eps_w, eps_b, out):
+    nc = tc.nc
+    with ExitStack() as ctx:
+        ctx.enter_context(tc.manual_schedule())
+        const = ctx.enter_context(tc.tile_pool(name="const", bufs=1))
+        xpool = ctx.enter_context(tc.tile_pool(name="xpool", bufs=1))
+        opool = ctx.enter_context(tc.tile_pool(name="opool", bufs=1))
+        gpool = ctx.enter_context(tc.tile_pool(name="gpool", bufs=3))
+        cpool = ctx.enter_context(tc.tile_pool(name="cpool", bufs=4))
+        tpsum = ctx.enter_context(tc.psum_pool(name="tpsum", bufs=6))
+        apsum = ctx.enter_context(tc.psum_pool(name="apsum", bufs=2))
+
+        xv = x.rearrange("(p j) k -> p (j k)", j=J)
+        ov = out.rearrange("(p j) n -> p (j n)", j=J)
+
+        zero_col = const.tile([P, 1], F32, name="zero_col")
+        one_col = const.tile([P, 1], F32, name="one_col")
+        warm = const.tile([P, 1], F32, name="warm")
+        brow = const.tile([P, 512], BF16, name="brow")
+        ones = const.tile([P, P], BF16, name="ones")
+        ident = const.tile([P, P], F32, name="ident")
+        nc.vector.memset(brow[:], 0.0)
+        nc.vector.memset(zero_col[:], 0.0)
+        nc.vector.memset(one_col[:], 1.0)
+        nc.vector.memset(ones[:], 1.0)
+        make_identity(nc, ident[:])
+        nc.scalar.dma_start(out=brow[0:1, N : 2 * N], in_=b_std)
+        nc.scalar.dma_start(out=brow[0:1, 0:N], in_=b_loc)
+        nc.scalar.dma_start(out=brow[0:1, 2 * N : 3 * N], in_=eps_b)
+        nc.scalar.activation(out=warm[:], in_=zero_col[:], func=ACT.Sigmoid)
+
+        ws = const.tile([P, K], BF16, name="ws")
+        we = const.tile([P, K], BF16, name="we")
+        wl = const.tile([P, K], BF16, name="wl")
+
+        def load_w(dst, src):
+            nc.sync.dma_start(
+                out=dst[:].rearrange("p (g c) -> p g c", g=2),
+                in_=src.rearrange("(g p t) n -> p g (t n)", g=2, p=P, t=4),
+            )
+
+        x_sb = [xpool.tile([P, CH], BF16, name="x%d" % c) for c in range(NCH)]
+
+        load_w(ws, w_std)
+        nc.sync.dma_start(out=x_sb[0][:, 0 : CH // 2], in_=xv[:, 0 : CH // 2])
+        nc.sync.dma_start(out=x_sb[0][:, CH // 2 : CH], in_=xv[:, CH // 2 : CH])
+        load_w(we, eps_w)
+        load_w(wl, w_loc)
+        for c in range(1, NCH):
+            nc.sync.dma_start(out=x_sb[c][:], in_=xv[:, c * CH : (c + 1) * CH])
+
+        banks = {}
+        grouped = {}
+        codes = {}
+        scales = {}
+        accs = {}
+        otiles = {}
+
+        def transposes(c):
+            xw = x_sb[c][:].bitcast(F32)
+            for jj in range(JC):
+                bank = tpsum.tile([P, 512], F32, name="xt")
+                for b in range(4):
+                    col = jj * 512 + (b // 2) * 256 + b % 2
+                    nc.tensor.transpose(bank[:, b * P : (b + 1) * P], xw[:, col : col + 255 : 2], ident[:])
+                banks[(c, jj)] = bank
+
+        def evacuate(c):
+            g_t = gpool.tile([P, CH], BF16, name="grouped", align_bytes=64)
+            grouped[c] = g_t
+            gw = g_t[:].bitcast(F32)
+            on_dve = dve_banks(c)
+            for jj in range(JC):
+                dst = gw[:, jj * 512 : (jj + 1) * 512].rearrange("p (g r u) -> p g r u", g=2, r=P, u=2)
+                src = banks[(c, jj)][:].rearrange("p (g u r) -> p g r u", g=2, u=2, r=P)
+                if jj in on_dve:
+                    nc.vector.tensor_copy(out=dst, in_=src)
+                else:
+                    nc.scalar.copy(out=dst, in_=src)
+
+        def quantise(c, part, parts):
+            if part == 0:
+                codes[c] = cpool.tile([P, CH // 4], U32, name="codes", align_bytes=64)
+                scales[c] = cpool.tile([P, CH // 4], U8, name="scales", align_bytes=64)
+            wd = CH // 4 // parts
+            nc.vector.quantize_mx(
+                out=codes[c][:, part * wd : (part + 1) * wd].bitcast(FP8X4),
+                scales=scales[c][:, part * wd : (part + 1) * wd],
+                in_=grouped[c][:, part * 4 * wd : (part + 1) * 4 * wd],
+            )
+
+        def multiply(c, first, count, pool, name):
+            acc = pool.tile([P, 512], F32, name=name)
+            accs[(c, first)] = acc
+            for i in range(count):
+                for g in range(2):
+                    col = ((first + i) * 2 + g) * P
+                    nc.tensor.matmul_mx(
+                        out=acc[:, i * N : (i + 1) * N],
+                        lhsT=codes[c][:, col : col + P].bitcast(FP8X4),
+                        lhsT_scale=scales[c][:, col : col + P],
+                        rhs=wcodes[:, g * N : (g + 1) * N].bitcast(FP8X4),
+                        rhs_scale=wscales[:, g * N : (g + 1) * N],
+                        start=(g == 0),
+                        stop=(g == 1),
+                    )
+
+        def finish(c, first, count):
+            j0 = c * JC + first
+            for (a, b) in STORES:
+                if a <= j0 < b:
+                    if a == j0:
+                        otiles[a] = opool.tile([P, (b - a) * N], F32, name="o%d" % a)
+                    o_t = otiles[a]
+                    off = (j0 - a) * N
+                    nc.vector.tensor_tensor(
+                        out=o_t[:, off : off + count * N].rearrange("p (j n) -> p j n", j=count),
+                        in0=accs[(c, first)][:, 0 : count * N].rearrange("p (j n) -> p j n", j=count),
+                        in1=bias[:].unsqueeze(1).to_broadcast([P, count, N]),
+                        op=ALU.add,
+                    )
+                    if j0 + count == b:
+                        nc.sync.dma_start(out=ov[:, a * N : b * N], in_=o_t[:])
+
+        na = const.tile([P, K], BF16, name="na")
+        ex = const.tile([P, K + N], F32, name="ex")
+        sg = const.tile([P, K + N], F32, name="sg")
+        ln = const.tile([P, K + N], F32, name="ln")
+        th = const.tile([P, K + N], F32, name="th")
+        wg = const.tile([P, K], BF16, name="wg", align_bytes=64)
+        wcodes = const.tile([P, K // 4], U32, name="wcodes", align_bytes=64)
+        wscales = const.tile([P, K // 4], U8, name="wscales", align_bytes=64)
+        bsb = const.tile([P, 3 * N], F32, name="bsb")
+        nb = const.tile([P, N], F32, name="nb")
+        bias = const.tile([P, N], F32, name="bias")
+        eb = ex[:, K : K + N]
+
+        bps = apsum.tile([P, 512], F32, name="acc")
+        nc.tensor.matmul(out=bps[:], lhsT=ones[:], rhs=brow[:], start=True, stop=True)
+
+        nc.vector.scalar_tensor_tensor(out=na[:], in0=ws[:], scalar=-1.0, in1=ws[:], op0=ALU.mult, op1=ALU.min)
+        nc.scalar.activation(out=sg[:, 0:K], in_=na[:], func=ACT.Sigmoid)
+        nc.vector.tensor_copy(out=bsb[:], in_=bps[:, 0 : 3 * N])
+        b_l = bsb[:, 0:N]
+        b_s = bsb[:, N : 2 * N]
+        b_e = bsb[:, 2 * N : 3 * N]
+        nc.vector.scalar_tensor_tensor(out=nb[:], in0=b_s, scalar=-1.0, in1=b_s, op0=ALU.mult, op1=ALU.min)
+        nc.scalar.activation(out=sg[:, K : K + N], in_=nb[:], func=ACT.Sigmoid)
+        nc.scalar.activation(out=ln[:], in_=sg[:], func=ACT.Ln, bias=one_col[:], scale=-1.0)
+        nc.scalar.activation(out=th[:], in_=ln[:], func=ACT.Tanh, scale=-0.5)
+
+        def softplus():
+            nc.vector.scalar_tensor_tensor(out=th[:], in0=sg[:], scalar=-2.0, in1=th[:], op0=ALU.add, op1=ALU.mult)
+            nc.vector.tensor_tensor(out=th[:], in0=th[:], in1=sg[:], op=ALU.add)
+            nc.vector.tensor_tensor(out=ex[:], in0=th[:], in1=ln[:], op=ALU.subtract)
+
+        def sample_w():
+            nc.vector.scalar_tensor_tensor(out=ex[:, 0:K], in0=ws[:], scalar=0.0, in1=ex[:, 0:K], op0=ALU.max, op1=ALU.add)
+            nc.vector.tensor_tensor(out=ex[:, 0:K], in0=ex[:, 0:K], in1=we[:], op=ALU.mult)
+            nc.vector.tensor_tensor(
+                out=wg[:].rearrange("p (g n t) -> p g n t", g=2, n=N, t=4),
+                in0=ex[:, 0:K].rearrange("p (g t n) -> p g n t", g=2, n=N, t=4),
+                in1=wl[:].rearrange("p (g t n) -> p g n t", g=2, n=N, t=4),
+                op=ALU.add,
+            )
+
+        def sample_b():
+            nc.vector.scalar_tensor_tensor(out=nb[:], in0=b_s, scalar=0.0, in1=eb, op0=ALU.max, op1=ALU.add)
+            nc.vector.tensor_tensor(out=nb[:], in0=nb[:], in1=b_e, op=ALU.mult)
+            nc.vector.tensor_tensor(out=bias[:], in0=nb[:], in1=b_l, op=ALU.add)
+
+        for c in range(NCH):
+            transposes(c)
+            if c >= M_LAG:
+                multiply(c - M_LAG, 0, JC, apsum, "acc")
+            evacuate(c)
+            if c >= O_LAG:
+                finish(c - O_LAG, 0, JC)
+            if c == 1:
+                softplus()
+                sample_w()
+                sample_b()
+                nc.vector.quantize_mx(out=wcodes[:].bitcast(FP8X4), scales=wscales[:], in_=wg[:])
+            if c >= 1:
+                quantise(c - 1, 0, 1)
+        L = NCH - 1
+        multiply(L - 2, 0, JC, apsum, "acc")
+        finish(L - 3, 0, JC)
+        quantise(L, 0, 2)
+        quantise(L, 1, 2)
+        multiply(L - 1, 0, JC, apsum, "acc")
+        finish(L - 2, 0, JC)
+        multiply(L, 0, 2, tpsum, "xt")
+        multiply(L, 2, 2, tpsum, "xt")
+        finish(L - 1, 0, JC)
+        finish(L, 0, 2)
+        finish(L, 2, 2)

@@ -1,3 +1,4 @@
+import math
 from contextlib import ExitStack
 
 import concourse.mybir as mybir
@@ -17,17 +18,17 @@ FLOPS = 2 * ROWS * K * N
 J = ROWS // P
 JC = 4
 NCH = J // JC
+LN2 = math.log(2.0)
 CH = JC * K
 STORES = [(0, 32), (32, 48), (48, 56), (56, 60), (60, 62), (62, 64)]
-M_LAG = 3
-O_LAG = 4
+M_LAG = 5
+HEAD = 2
+XBUFS = 8
 
 
 def dve_banks(c):
-    if c == 0:
-        return (0, 1, 2)
-    if c in (6, 11):
-        return (0,)
+    if c < HEAD:
+        return (0, 1, 2, 3) if c == 0 else (0, 1)
     return ()
 
 
@@ -36,10 +37,10 @@ def tile_bayesiandenselayer_t_kernel(tc, x, w_loc, w_std, b_loc, b_std, eps_w, e
     with ExitStack() as ctx:
         ctx.enter_context(tc.manual_schedule())
         const = ctx.enter_context(tc.tile_pool(name="const", bufs=1))
-        xpool = ctx.enter_context(tc.tile_pool(name="xpool", bufs=1))
+        xpool = ctx.enter_context(tc.tile_pool(name="xpool", bufs=XBUFS))
         opool = ctx.enter_context(tc.tile_pool(name="opool", bufs=1))
-        gpool = ctx.enter_context(tc.tile_pool(name="gpool", bufs=3))
-        cpool = ctx.enter_context(tc.tile_pool(name="cpool", bufs=4))
+        gpool = ctx.enter_context(tc.tile_pool(name="gpool", bufs=5))
+        cpool = ctx.enter_context(tc.tile_pool(name="cpool", bufs=M_LAG + 2))
         tpsum = ctx.enter_context(tc.psum_pool(name="tpsum", bufs=6))
         apsum = ctx.enter_context(tc.psum_pool(name="apsum", bufs=2))
 
@@ -47,20 +48,18 @@ def tile_bayesiandenselayer_t_kernel(tc, x, w_loc, w_std, b_loc, b_std, eps_w, e
         ov = out.rearrange("(p j) n -> p (j n)", j=J)
 
         zero_col = const.tile([P, 1], F32, name="zero_col")
+        shift = const.tile([P, 1], F32, name="shift")
         one_col = const.tile([P, 1], F32, name="one_col")
         warm = const.tile([P, 1], F32, name="warm")
-        brow = const.tile([P, 512], BF16, name="brow")
+        brow = const.tile([P, 3 * N], BF16, name="brow")
         ones = const.tile([P, P], BF16, name="ones")
         ident = const.tile([P, P], F32, name="ident")
         nc.vector.memset(brow[:], 0.0)
         nc.vector.memset(zero_col[:], 0.0)
         nc.vector.memset(one_col[:], 1.0)
+        nc.vector.tensor_scalar_add(out=shift[:], in0=zero_col[:], scalar1=-LN2)
         nc.vector.memset(ones[:], 1.0)
         make_identity(nc, ident[:])
-        nc.scalar.dma_start(out=brow[0:1, N : 2 * N], in_=b_std)
-        nc.scalar.dma_start(out=brow[0:1, 0:N], in_=b_loc)
-        nc.scalar.dma_start(out=brow[0:1, 2 * N : 3 * N], in_=eps_b)
-        nc.scalar.activation(out=warm[:], in_=zero_col[:], func=ACT.Sigmoid)
 
         ws = const.tile([P, K], BF16, name="ws")
         we = const.tile([P, K], BF16, name="we")
@@ -72,15 +71,25 @@ def tile_bayesiandenselayer_t_kernel(tc, x, w_loc, w_std, b_loc, b_std, eps_w, e
                 in_=src.rearrange("(g p t) n -> p g (t n)", g=2, p=P, t=4),
             )
 
-        x_sb = [xpool.tile([P, CH], BF16, name="x%d" % c) for c in range(NCH)]
+        x_sb = {}
+
+        def load_x(c, parts):
+            x_sb[c] = xpool.tile([P, CH], BF16, name="x")
+            wd = CH // parts
+            for i in range(parts):
+                nc.sync.dma_start(out=x_sb[c][:, i * wd : (i + 1) * wd], in_=xv[:, c * CH + i * wd : c * CH + (i + 1) * wd])
 
         load_w(ws, w_std)
-        nc.sync.dma_start(out=x_sb[0][:, 0 : CH // 2], in_=xv[:, 0 : CH // 2])
-        nc.sync.dma_start(out=x_sb[0][:, CH // 2 : CH], in_=xv[:, CH // 2 : CH])
-        load_w(we, eps_w)
-        load_w(wl, w_loc)
-        for c in range(1, NCH):
-            nc.sync.dma_start(out=x_sb[c][:], in_=xv[:, c * CH : (c + 1) * CH])
+        nc.scalar.dma_start(out=brow[0:1, N : 2 * N], in_=b_std)
+        nc.scalar.dma_start(out=brow[0:1, 0:N], in_=b_loc)
+        nc.scalar.dma_start(out=brow[0:1, 2 * N : 3 * N], in_=eps_b)
+        nc.scalar.activation(out=warm[:], in_=zero_col[:], func=ACT.Ln, bias=one_col[:], scale=1.0)
+        load_x(0, 2)
+        for c in range(1, XBUFS):
+            load_x(c, 1)
+            if c == 1:
+                load_w(we, eps_w)
+                load_w(wl, w_loc)
 
         banks = {}
         grouped = {}
@@ -98,17 +107,16 @@ def tile_bayesiandenselayer_t_kernel(tc, x, w_loc, w_std, b_loc, b_std, eps_w, e
                     nc.tensor.transpose(bank[:, b * P : (b + 1) * P], xw[:, col : col + 255 : 2], ident[:])
                 banks[(c, jj)] = bank
 
-        def evacuate(c):
-            g_t = gpool.tile([P, CH], BF16, name="grouped", align_bytes=64)
-            grouped[c] = g_t
-            gw = g_t[:].bitcast(F32)
-            on_dve = dve_banks(c)
+        def evacuate(c, on_dve):
+            if c not in grouped:
+                grouped[c] = gpool.tile([P, CH], BF16, name="grouped", align_bytes=64)
+            gw = grouped[c][:].bitcast(F32)
             for jj in range(JC):
                 dst = gw[:, jj * 512 : (jj + 1) * 512].rearrange("p (g r u) -> p g r u", g=2, r=P, u=2)
                 src = banks[(c, jj)][:].rearrange("p (g u r) -> p g r u", g=2, u=2, r=P)
-                if jj in on_dve:
+                if on_dve and jj in dve_banks(c):
                     nc.vector.tensor_copy(out=dst, in_=src)
-                else:
+                if not on_dve and jj not in dve_banks(c):
                     nc.scalar.copy(out=dst, in_=src)
 
         def quantise(c, part, parts):
@@ -155,76 +163,103 @@ def tile_bayesiandenselayer_t_kernel(tc, x, w_loc, w_std, b_loc, b_std, eps_w, e
                     if j0 + count == b:
                         nc.sync.dma_start(out=ov[:, a * N : b * N], in_=o_t[:])
 
-        na = const.tile([P, K], BF16, name="na")
-        ex = const.tile([P, K + N], F32, name="ex")
-        sg = const.tile([P, K + N], F32, name="sg")
+        nv = const.tile([P, K], BF16, name="nv")
         ln = const.tile([P, K + N], F32, name="ln")
+        sg = const.tile([P, K + N], F32, name="sg")
         th = const.tile([P, K + N], F32, name="th")
+        ex = const.tile([P, K + N], F32, name="ex")
         wg = const.tile([P, K], BF16, name="wg", align_bytes=64)
         wcodes = const.tile([P, K // 4], U32, name="wcodes", align_bytes=64)
         wscales = const.tile([P, K // 4], U8, name="wscales", align_bytes=64)
         bsb = const.tile([P, 3 * N], F32, name="bsb")
         nb = const.tile([P, N], F32, name="nb")
         bias = const.tile([P, N], F32, name="bias")
-        eb = ex[:, K : K + N]
-
-        bps = apsum.tile([P, 512], F32, name="acc")
-        nc.tensor.matmul(out=bps[:], lhsT=ones[:], rhs=brow[:], start=True, stop=True)
-
-        nc.vector.scalar_tensor_tensor(out=na[:], in0=ws[:], scalar=-1.0, in1=ws[:], op0=ALU.mult, op1=ALU.min)
-        nc.scalar.activation(out=sg[:, 0:K], in_=na[:], func=ACT.Sigmoid)
-        nc.vector.tensor_copy(out=bsb[:], in_=bps[:, 0 : 3 * N])
         b_l = bsb[:, 0:N]
         b_s = bsb[:, N : 2 * N]
         b_e = bsb[:, 2 * N : 3 * N]
+
+        bps = apsum.tile([P, 512], F32, name="acc")
+        nc.tensor.matmul(out=bps[:, 0 : 3 * N], lhsT=ones[:], rhs=brow[:], start=True, stop=True)
+        nc.vector.scalar_tensor_tensor(out=nv[:], in0=ws[:], scalar=-1.0, in1=ws[:], op0=ALU.mult, op1=ALU.min)
+        nc.scalar.activation(out=ex[:, 0:K], in_=nv[:], func=ACT.Exp)
+        nc.vector.tensor_copy(out=bsb[:], in_=bps[:, 0 : 3 * N])
         nc.vector.scalar_tensor_tensor(out=nb[:], in0=b_s, scalar=-1.0, in1=b_s, op0=ALU.mult, op1=ALU.min)
-        nc.scalar.activation(out=sg[:, K : K + N], in_=nb[:], func=ACT.Sigmoid)
-        nc.scalar.activation(out=ln[:], in_=sg[:], func=ACT.Ln, bias=one_col[:], scale=-1.0)
-        nc.scalar.activation(out=th[:], in_=ln[:], func=ACT.Tanh, scale=-0.5)
+        nc.scalar.activation(out=ex[:, K : K + N], in_=nb[:], func=ACT.Exp)
+        nc.scalar.activation(out=ln[:], in_=ex[:], func=ACT.Ln, bias=one_col[:], scale=1.0)
+        nc.scalar.activation(out=sg[:, 0:K], in_=nv[:], func=ACT.Sigmoid, bias=shift[:], scale=1.0)
+        nc.scalar.activation(out=sg[:, K : K + N], in_=nb[:], func=ACT.Sigmoid, bias=shift[:], scale=1.0)
+        nc.scalar.activation(out=th[:], in_=ln[:], func=ACT.Tanh, scale=0.5)
 
-        def softplus():
-            nc.vector.scalar_tensor_tensor(out=th[:], in0=sg[:], scalar=-2.0, in1=th[:], op0=ALU.add, op1=ALU.mult)
-            nc.vector.tensor_tensor(out=th[:], in0=th[:], in1=sg[:], op=ALU.add)
-            nc.vector.tensor_tensor(out=ex[:], in0=th[:], in1=ln[:], op=ALU.subtract)
+        def tt(out, in0, in1, op):
+            nc.vector.tensor_tensor(out=out, in0=in0, in1=in1, op=op)
 
-        def sample_w():
-            nc.vector.scalar_tensor_tensor(out=ex[:, 0:K], in0=ws[:], scalar=0.0, in1=ex[:, 0:K], op0=ALU.max, op1=ALU.add)
-            nc.vector.tensor_tensor(out=ex[:, 0:K], in0=ex[:, 0:K], in1=we[:], op=ALU.mult)
-            nc.vector.tensor_tensor(
-                out=wg[:].rearrange("p (g n t) -> p g n t", g=2, n=N, t=4),
-                in0=ex[:, 0:K].rearrange("p (g t n) -> p g n t", g=2, n=N, t=4),
-                in1=wl[:].rearrange("p (g t n) -> p g n t", g=2, n=N, t=4),
-                op=ALU.add,
+        def stt(out, in0, scalar, in1, op0, op1):
+            nc.vector.scalar_tensor_tensor(out=out, in0=in0, scalar=scalar, in1=in1, op0=op0, op1=op1)
+
+        def w_relu():
+            stt(ex[:, 0:K], ws[:], 0.0, ln[:, 0:K], ALU.max, ALU.add)
+
+        def w_diff():
+            tt(sg[:], sg[:], th[:], ALU.subtract)
+
+        def w_softplus():
+            stt(ex[:, 0:K], sg[:, 0:K], 2.0, ex[:, 0:K], ALU.mult, ALU.add)
+
+        def w_eps():
+            tt(ex[:, 0:K], ex[:, 0:K], we[:], ALU.mult)
+
+        def w_loc_add():
+            tt(
+                wg[:].rearrange("p (g n t) -> p g n t", g=2, n=N, t=4),
+                ex[:, 0:K].rearrange("p (g t n) -> p g n t", g=2, n=N, t=4),
+                wl[:].rearrange("p (g t n) -> p g n t", g=2, n=N, t=4),
+                ALU.add,
             )
 
-        def sample_b():
-            nc.vector.scalar_tensor_tensor(out=nb[:], in0=b_s, scalar=0.0, in1=eb, op0=ALU.max, op1=ALU.add)
-            nc.vector.tensor_tensor(out=nb[:], in0=nb[:], in1=b_e, op=ALU.mult)
-            nc.vector.tensor_tensor(out=bias[:], in0=nb[:], in1=b_l, op=ALU.add)
+        def w_quantise():
+            nc.vector.quantize_mx(out=wcodes[:].bitcast(FP8X4), scales=wscales[:], in_=wg[:])
 
+        def sample_b():
+            pool = nc.gpsimd
+            pool.tensor_scalar(out=nb[:], in0=b_s, scalar1=0.0, scalar2=0.0, op0=ALU.max, op1=ALU.add)
+            pool.tensor_tensor(out=nb[:], in0=nb[:], in1=ln[:, K : K + N], op=ALU.add)
+            pool.tensor_scalar(out=bias[:], in0=sg[:, K : K + N], scalar1=2.0, scalar2=0.0, op0=ALU.mult, op1=ALU.add)
+            pool.tensor_tensor(out=bias[:], in0=bias[:], in1=nb[:], op=ALU.add)
+            pool.tensor_tensor(out=bias[:], in0=bias[:], in1=b_e, op=ALU.mult)
+            pool.tensor_tensor(out=bias[:], in0=bias[:], in1=b_l, op=ALU.add)
+
+        LAST = NCH - 1
         for c in range(NCH):
             transposes(c)
+            if c + XBUFS < NCH:
+                load_x(c + XBUFS, 1)
+            evacuate(c, False)
             if c >= M_LAG:
                 multiply(c - M_LAG, 0, JC, apsum, "acc")
-            evacuate(c)
-            if c >= O_LAG:
-                finish(c - O_LAG, 0, JC)
-            if c == 1:
-                softplus()
-                sample_w()
-                sample_b()
-                nc.vector.quantize_mx(out=wcodes[:].bitcast(FP8X4), scales=wscales[:], in_=wg[:])
+            evacuate(c, True)
+            if c > M_LAG:
+                finish(c - M_LAG - 1, 0, JC)
             if c >= 1:
                 quantise(c - 1, 0, 1)
-        L = NCH - 1
-        multiply(L - 2, 0, JC, apsum, "acc")
-        finish(L - 3, 0, JC)
-        quantise(L, 0, 2)
-        quantise(L, 1, 2)
-        multiply(L - 1, 0, JC, apsum, "acc")
-        finish(L - 2, 0, JC)
-        multiply(L, 0, 2, tpsum, "xt")
-        multiply(L, 2, 2, tpsum, "xt")
-        finish(L - 1, 0, JC)
-        finish(L, 0, 2)
-        finish(L, 2, 2)
+            if c == 0:
+                w_relu()
+            if c == 1:
+                w_diff()
+                w_softplus()
+            if c == 2:
+                w_eps()
+                w_loc_add()
+                w_quantise()
+            if c == 3:
+                sample_b()
+        for c in range(NCH - M_LAG, LAST):
+            multiply(c, 0, JC, apsum, "acc")
+            finish(c - 1, 0, JC)
+            if c == NCH - M_LAG:
+                quantise(LAST, 0, 2)
+                quantise(LAST, 1, 2)
+        multiply(LAST, 0, 2, tpsum, "xt")
+        multiply(LAST, 2, 2, tpsum, "xt")
+        finish(LAST - 1, 0, JC)
+        finish(LAST, 0, 2)
+        finish(LAST, 2, 2)

@@ -20,7 +20,7 @@ JC = 4
 NCH = J // JC
 LN2 = math.log(2.0)
 CH = JC * K
-STORES = [(0, 32), (32, 48), (48, 56), (56, 60), (60, 62), (62, 64)]
+STORES = [(0, 32), (32, 44), (44, 52), (52, 56), (56, 60), (60, 62), (62, 64)]
 M_LAG = 5
 HEAD = 2
 XBUFS = 8
@@ -32,6 +32,10 @@ def dve_banks(c):
     return ()
 
 
+def gathered(c):
+    return (1, 3) if c >= 7 else ()
+
+
 def tile_bayesiandenselayer_t_kernel(tc, x, w_loc, w_std, b_loc, b_std, eps_w, eps_b, out):
     nc = tc.nc
     with ExitStack() as ctx:
@@ -39,6 +43,7 @@ def tile_bayesiandenselayer_t_kernel(tc, x, w_loc, w_std, b_loc, b_std, eps_w, e
         const = ctx.enter_context(tc.tile_pool(name="const", bufs=1))
         xpool = ctx.enter_context(tc.tile_pool(name="xpool", bufs=XBUFS))
         opool = ctx.enter_context(tc.tile_pool(name="opool", bufs=1))
+        rpool = ctx.enter_context(tc.tile_pool(name="rpool", bufs=3))
         gpool = ctx.enter_context(tc.tile_pool(name="gpool", bufs=5))
         cpool = ctx.enter_context(tc.tile_pool(name="cpool", bufs=M_LAG + 2))
         tpsum = ctx.enter_context(tc.psum_pool(name="tpsum", bufs=6))
@@ -78,11 +83,12 @@ def tile_bayesiandenselayer_t_kernel(tc, x, w_loc, w_std, b_loc, b_std, eps_w, e
             wd = CH // parts
             for i in range(parts):
                 nc.sync.dma_start(out=x_sb[c][:, i * wd : (i + 1) * wd], in_=xv[:, c * CH + i * wd : c * CH + (i + 1) * wd])
+                if c == 0 and i == 0:
+                    nc.sync.dma_start(out=brow[0:1, N : 2 * N], in_=b_std)
+                    nc.sync.dma_start(out=brow[0:1, 0:N], in_=b_loc)
+                    nc.sync.dma_start(out=brow[0:1, 2 * N : 3 * N], in_=eps_b)
 
         load_w(ws, w_std)
-        nc.scalar.dma_start(out=brow[0:1, N : 2 * N], in_=b_std)
-        nc.scalar.dma_start(out=brow[0:1, 0:N], in_=b_loc)
-        nc.scalar.dma_start(out=brow[0:1, 2 * N : 3 * N], in_=eps_b)
         nc.scalar.activation(out=warm[:], in_=zero_col[:], func=ACT.Ln, bias=one_col[:], scale=1.0)
         load_x(0, 2)
         for c in range(1, XBUFS):
@@ -92,19 +98,33 @@ def tile_bayesiandenselayer_t_kernel(tc, x, w_loc, w_std, b_loc, b_std, eps_w, e
                 load_w(wl, w_loc)
 
         banks = {}
+        gath = {}
         grouped = {}
         codes = {}
         scales = {}
         accs = {}
         otiles = {}
 
+        def gather(c):
+            for jj in gathered(c):
+                t = rpool.tile([P, 512], F32, name="gath")
+                gath[(c, jj)] = t
+                nc.vector.tensor_copy(
+                    out=t[:].rearrange("p (g u r) -> p g u r", g=2, u=2, r=P),
+                    in_=x_sb[c][:].bitcast(F32)[:, jj * 512 : (jj + 1) * 512].rearrange("p (g r u) -> p g u r", g=2, r=P, u=2),
+                )
+
         def transposes(c):
             xw = x_sb[c][:].bitcast(F32)
             for jj in range(JC):
                 bank = tpsum.tile([P, 512], F32, name="xt")
                 for b in range(4):
-                    col = jj * 512 + (b // 2) * 256 + b % 2
-                    nc.tensor.transpose(bank[:, b * P : (b + 1) * P], xw[:, col : col + 255 : 2], ident[:])
+                    if jj in gathered(c):
+                        words = gath[(c, jj)][:, b * P : (b + 1) * P]
+                    else:
+                        col = jj * 512 + (b // 2) * 256 + b % 2
+                        words = xw[:, col : col + 255 : 2]
+                    nc.tensor.transpose(bank[:, b * P : (b + 1) * P], words, ident[:])
                 banks[(c, jj)] = bank
 
         def evacuate(c, on_dve):
@@ -229,16 +249,22 @@ def tile_bayesiandenselayer_t_kernel(tc, x, w_loc, w_std, b_loc, b_std, eps_w, e
             pool.tensor_tensor(out=bias[:], in0=bias[:], in1=b_l, op=ALU.add)
 
         LAST = NCH - 1
+        made = 0
+        done = 0
         for c in range(NCH):
             transposes(c)
             if c + XBUFS < NCH:
                 load_x(c + XBUFS, 1)
             evacuate(c, False)
-            if c >= M_LAG:
-                multiply(c - M_LAG, 0, JC, apsum, "acc")
-            evacuate(c, True)
-            if c > M_LAG:
-                finish(c - M_LAG - 1, 0, JC)
+            ready = made
+            while made <= c - (5 if c < 8 else 4 if c < 10 else 3 if c < 13 else 2):
+                multiply(made, 0, JC, apsum, "acc")
+                made += 1
+            if c < LAST:
+                evacuate(c, True)
+            while done < ready:
+                finish(done, 0, JC)
+                done += 1
             if c >= 1:
                 quantise(c - 1, 0, 1)
             if c == 0:
@@ -252,14 +278,20 @@ def tile_bayesiandenselayer_t_kernel(tc, x, w_loc, w_std, b_loc, b_std, eps_w, e
                 w_quantise()
             if c == 3:
                 sample_b()
-        for c in range(NCH - M_LAG, LAST):
-            multiply(c, 0, JC, apsum, "acc")
-            finish(c - 1, 0, JC)
-            if c == NCH - M_LAG:
-                quantise(LAST, 0, 2)
-                quantise(LAST, 1, 2)
+            if c >= 5 and c + 2 < NCH:
+                gather(c + 2)
+        evacuate(LAST, True)
+        for part in range(2):
+            quantise(LAST, part, 2)
+        while made < LAST:
+            multiply(made, 0, JC, apsum, "acc")
+            made += 1
+            finish(done, 0, JC)
+            done += 1
         multiply(LAST, 0, 2, tpsum, "xt")
         multiply(LAST, 2, 2, tpsum, "xt")
-        finish(LAST - 1, 0, JC)
+        while done < LAST:
+            finish(done, 0, JC)
+            done += 1
         finish(LAST, 0, 2)
         finish(LAST, 2, 2)

@@ -89,7 +89,7 @@ def tile_bayesiandenselayer_t_kernel(tc, x, w_loc, w_std, b_loc, b_std, eps_w, e
                     nc.sync.dma_start(out=brow[0:1, 2 * N : 3 * N], in_=eps_b)
 
         load_w(ws, w_std)
-        nc.scalar.activation(out=warm[:], in_=zero_col[:], func=ACT.Ln, bias=one_col[:], scale=1.0)
+        nc.scalar.activation(out=warm[:], in_=zero_col[:], func=ACT.Sigmoid)
         load_x(0, 2)
         for c in range(1, XBUFS):
             load_x(c, 1)
@@ -201,14 +201,14 @@ def tile_bayesiandenselayer_t_kernel(tc, x, w_loc, w_std, b_loc, b_std, eps_w, e
         bps = apsum.tile([P, 512], F32, name="acc")
         nc.tensor.matmul(out=bps[:, 0 : 3 * N], lhsT=ones[:], rhs=brow[:], start=True, stop=True)
         nc.vector.scalar_tensor_tensor(out=nv[:], in0=ws[:], scalar=-1.0, in1=ws[:], op0=ALU.mult, op1=ALU.min)
-        nc.scalar.activation(out=ex[:, 0:K], in_=nv[:], func=ACT.Exp)
+        nc.scalar.activation(out=ex[:, 0:K], in_=nv[:], func=ACT.Sigmoid)
+        nc.scalar.activation(out=sg[:, 0:K], in_=nv[:], func=ACT.Sigmoid, bias=shift[:], scale=1.0)
         nc.vector.tensor_copy(out=bsb[:], in_=bps[:, 0 : 3 * N])
         nc.vector.scalar_tensor_tensor(out=nb[:], in0=b_s, scalar=-1.0, in1=b_s, op0=ALU.mult, op1=ALU.min)
-        nc.scalar.activation(out=ex[:, K : K + N], in_=nb[:], func=ACT.Exp)
-        nc.scalar.activation(out=ln[:], in_=ex[:], func=ACT.Ln, bias=one_col[:], scale=1.0)
-        nc.scalar.activation(out=sg[:, 0:K], in_=nv[:], func=ACT.Sigmoid, bias=shift[:], scale=1.0)
+        nc.scalar.activation(out=ex[:, K : K + N], in_=nb[:], func=ACT.Sigmoid)
         nc.scalar.activation(out=sg[:, K : K + N], in_=nb[:], func=ACT.Sigmoid, bias=shift[:], scale=1.0)
-        nc.scalar.activation(out=th[:], in_=ln[:], func=ACT.Tanh, scale=0.5)
+        nc.scalar.activation(out=ln[:], in_=ex[:], func=ACT.Ln, bias=one_col[:], scale=-1.0)
+        nc.scalar.activation(out=th[:], in_=ln[:], func=ACT.Tanh, scale=-0.5)
 
         def tt(out, in0, in1, op):
             nc.vector.tensor_tensor(out=out, in0=in0, in1=in1, op=op)
@@ -217,7 +217,7 @@ def tile_bayesiandenselayer_t_kernel(tc, x, w_loc, w_std, b_loc, b_std, eps_w, e
             nc.vector.scalar_tensor_tensor(out=out, in0=in0, scalar=scalar, in1=in1, op0=op0, op1=op1)
 
         def w_relu():
-            stt(ex[:, 0:K], ws[:], 0.0, ln[:, 0:K], ALU.max, ALU.add)
+            stt(ex[:, 0:K], ws[:], 0.0, ln[:, 0:K], ALU.max, ALU.subtract)
 
         def w_diff():
             tt(sg[:], sg[:], th[:], ALU.subtract)
@@ -239,14 +239,17 @@ def tile_bayesiandenselayer_t_kernel(tc, x, w_loc, w_std, b_loc, b_std, eps_w, e
         def w_quantise():
             nc.vector.quantize_mx(out=wcodes[:].bitcast(FP8X4), scales=wscales[:], in_=wg[:])
 
-        def sample_b():
-            pool = nc.gpsimd
-            pool.tensor_scalar(out=nb[:], in0=b_s, scalar1=0.0, scalar2=0.0, op0=ALU.max, op1=ALU.add)
-            pool.tensor_tensor(out=nb[:], in0=nb[:], in1=ln[:, K : K + N], op=ALU.add)
-            pool.tensor_scalar(out=bias[:], in0=sg[:, K : K + N], scalar1=2.0, scalar2=0.0, op0=ALU.mult, op1=ALU.add)
-            pool.tensor_tensor(out=bias[:], in0=bias[:], in1=nb[:], op=ALU.add)
-            pool.tensor_tensor(out=bias[:], in0=bias[:], in1=b_e, op=ALU.mult)
-            pool.tensor_tensor(out=bias[:], in0=bias[:], in1=b_l, op=ALU.add)
+        def b_relu():
+            stt(bias[:], b_s, 0.0, ln[:, K : K + N], ALU.max, ALU.subtract)
+
+        def b_softplus():
+            stt(bias[:], sg[:, K : K + N], 2.0, bias[:], ALU.mult, ALU.add)
+
+        def b_eps():
+            tt(bias[:], bias[:], b_e, ALU.mult)
+
+        def b_loc_add():
+            tt(bias[:], bias[:], b_l, ALU.add)
 
         LAST = NCH - 1
         made = 0
@@ -257,31 +260,33 @@ def tile_bayesiandenselayer_t_kernel(tc, x, w_loc, w_std, b_loc, b_std, eps_w, e
                 load_x(c + XBUFS, 1)
             evacuate(c, False)
             ready = made
-            while made <= c - (5 if c < 8 else 4 if c < 10 else 3 if c < 13 else 2):
+            while made <= c - (5 if c < 8 else 4 if c < 11 else 3):
                 multiply(made, 0, JC, apsum, "acc")
                 made += 1
-            if c < LAST:
-                evacuate(c, True)
+            evacuate(c, True)
             while done < ready:
                 finish(done, 0, JC)
                 done += 1
             if c >= 1:
                 quantise(c - 1, 0, 1)
-            if c == 0:
-                w_relu()
             if c == 1:
+                w_relu()
                 w_diff()
+                b_relu()
                 w_softplus()
+                b_softplus()
             if c == 2:
                 w_eps()
+                b_eps()
                 w_loc_add()
+                b_loc_add()
                 w_quantise()
-            if c == 3:
-                sample_b()
             if c >= 5 and c + 2 < NCH:
                 gather(c + 2)
-        evacuate(LAST, True)
         for part in range(2):
+            if done < made:
+                finish(done, 0, JC)
+                done += 1
             quantise(LAST, part, 2)
         while made < LAST:
             multiply(made, 0, JC, apsum, "acc")

@@ -260,7 +260,7 @@ def tile_bayesiandenselayer_t_kernel(tc, x, w_loc, w_std, b_loc, b_std, eps_w, e
                 load_x(c + XBUFS, 1)
             evacuate(c, False)
             ready = made
-            while made <= c - (5 if c < 8 else 4 if c < 11 else 3):
+            while c % 2 == 1 and made <= c - (4):
                 multiply(made, 0, JC, apsum, "acc")
                 made += 1
             evacuate(c, True)

@@ -33,7 +33,7 @@ def dve_banks(c):
 
 
 def gathered(c):
-    return (1, 3) if c >= 7 else ()
+    return () if c < 7 else (0, 1) if c % 2 else (2, 3)
 
 
 def tile_bayesiandenselayer_t_kernel(tc, x, w_loc, w_std, b_loc, b_std, eps_w, eps_b, out):
@@ -43,7 +43,7 @@ def tile_bayesiandenselayer_t_kernel(tc, x, w_loc, w_std, b_loc, b_std, eps_w, e
         const = ctx.enter_context(tc.tile_pool(name="const", bufs=1))
         xpool = ctx.enter_context(tc.tile_pool(name="xpool", bufs=XBUFS))
         opool = ctx.enter_context(tc.tile_pool(name="opool", bufs=1))
-        rpool = ctx.enter_context(tc.tile_pool(name="rpool", bufs=3))
+        rpool = ctx.enter_context(tc.tile_pool(name="rpool", bufs=6))
         gpool = ctx.enter_context(tc.tile_pool(name="gpool", bufs=5))
         cpool = ctx.enter_context(tc.tile_pool(name="cpool", bufs=M_LAG + 2))
         tpsum = ctx.enter_context(tc.psum_pool(name="tpsum", bufs=6))
@@ -283,16 +283,13 @@ def tile_bayesiandenselayer_t_kernel(tc, x, w_loc, w_std, b_loc, b_std, eps_w, e
                 w_quantise()
             if c >= 5 and c + 2 < NCH:
                 gather(c + 2)
-        for part in range(2):
-            if done < made:
-                finish(done, 0, JC)
-                done += 1
-            quantise(LAST, part, 2)
         while made < LAST:
-            multiply(made, 0, JC, apsum, "acc")
+            multiply(made, 0, JC, tpsum, "xt")
             made += 1
+        for part in range(2):
             finish(done, 0, JC)
             done += 1
+            quantise(LAST, part, 2)
         multiply(LAST, 0, 2, tpsum, "xt")
         multiply(LAST, 2, 2, tpsum, "xt")
         while done < LAST:

@@ -90,10 +90,10 @@ def tile_bayesiandenselayer_t_kernel(tc, x, w_loc, w_std, b_loc, b_std, eps_w, e
 
         load_w(ws, w_std)
         nc.scalar.activation(out=warm[:], in_=zero_col[:], func=ACT.Sigmoid)
-        load_x(0, 2)
+        load_x(0, 4)
         for c in range(1, XBUFS):
             load_x(c, 1)
-            if c == 1:
+            if c == 3:
                 load_w(we, eps_w)
                 load_w(wl, w_loc)
 

import math
from contextlib import ExitStack

import concourse.mybir as mybir
from concourse.masks import make_identity

F32 = mybir.dt.float32
BF16 = mybir.dt.bfloat16
U32 = mybir.dt.uint32
U8 = mybir.dt.uint8
FP8X4 = mybir.dt.float8_e4m3fn_x4
ALU = mybir.AluOpType
ACT = mybir.ActivationFunctionType

P = 128
ROWS, K, N = 8192, 1024, 128
FLOPS = 2 * ROWS * K * N
J = ROWS // P
JC = 4
NCH = J // JC
LN2 = math.log(2.0)
CH = JC * K
STORES = [(0, 32), (32, 44), (44, 52), (52, 56), (56, 60), (60, 62), (62, 64)]
M_LAG = 5
HEAD = 2
XBUFS = 8


def dve_banks(c):
    if c < HEAD:
        return (0, 1, 2, 3) if c == 0 else (0, 1)
    return ()


def gathered(c):
    return () if c < 7 else (0, 1) if c % 2 else (2, 3)


def tile_bayesiandenselayer_t_kernel(tc, x, w_loc, w_std, b_loc, b_std, eps_w, eps_b, out):
    nc = tc.nc
    with ExitStack() as ctx:
        ctx.enter_context(tc.manual_schedule())
        const = ctx.enter_context(tc.tile_pool(name="const", bufs=1))
        xpool = ctx.enter_context(tc.tile_pool(name="xpool", bufs=XBUFS))
        opool = ctx.enter_context(tc.tile_pool(name="opool", bufs=1))
        rpool = ctx.enter_context(tc.tile_pool(name="rpool", bufs=6))
        gpool = ctx.enter_context(tc.tile_pool(name="gpool", bufs=5))
        cpool = ctx.enter_context(tc.tile_pool(name="cpool", bufs=M_LAG + 2))
        tpsum = ctx.enter_context(tc.psum_pool(name="tpsum", bufs=6))
        apsum = ctx.enter_context(tc.psum_pool(name="apsum", bufs=2))

        xv = x.rearrange("(p j) k -> p (j k)", j=J)
        ov = out.rearrange("(p j) n -> p (j n)", j=J)

        zero_col = const.tile([P, 1], F32, name="zero_col")
        shift = const.tile([P, 1], F32, name="shift")
        one_col = const.tile([P, 1], F32, name="one_col")
        warm = const.tile([P, 1], F32, name="warm")
        brow = const.tile([P, 3 * N], BF16, name="brow")
        ones = const.tile([P, P], BF16, name="ones")
        ident = const.tile([P, P], F32, name="ident")
        nc.vector.memset(brow[:], 0.0)
        nc.vector.memset(zero_col[:], 0.0)
        nc.vector.memset(one_col[:], 1.0)
        nc.vector.tensor_scalar_add(out=shift[:], in0=zero_col[:], scalar1=-LN2)
        nc.vector.memset(ones[:], 1.0)
        make_identity(nc, ident[:])

        ws = const.tile([P, K], BF16, name="ws")
        we = const.tile([P, K], BF16, name="we")
        wl = const.tile([P, K], BF16, name="wl")

        def load_w(dst, src):
            nc.sync.dma_start(
                out=dst[:].rearrange("p (g c) -> p g c", g=2),
                in_=src.rearrange("(g p t) n -> p g (t n)", g=2, p=P, t=4),
            )

        x_sb = {}

        def load_x(c, parts):
            x_sb[c] = xpool.tile([P, CH], BF16, name="x")
            wd = CH // parts
            for i in range(parts):
                nc.sync.dma_start(out=x_sb[c][:, i * wd : (i + 1) * wd], in_=xv[:, c * CH + i * wd : c * CH + (i + 1) * wd])
                if c == 0 and i == 0:
                    nc.sync.dma_start(out=brow[0:1, N : 2 * N], in_=b_std)
                    nc.sync.dma_start(out=brow[0:1, 0:N], in_=b_loc)
                    nc.sync.dma_start(out=brow[0:1, 2 * N : 3 * N], in_=eps_b)

        load_w(ws, w_std)
        nc.scalar.activation(out=warm[:], in_=zero_col[:], func=ACT.Sigmoid)
        load_x(0, 4)
        for c in range(1, XBUFS):
            load_x(c, 1)
            if c == 3:
                load_w(we, eps_w)
                load_w(wl, w_loc)

        banks = {}
        gath = {}
        grouped = {}
        codes = {}
        scales = {}
        accs = {}
        otiles = {}

        def gather(c):
            for jj in gathered(c):
                t = rpool.tile([P, 512], F32, name="gath")
                gath[(c, jj)] = t
                nc.vector.tensor_copy(
                    out=t[:].rearrange("p (g u r) -> p g u r", g=2, u=2, r=P),
                    in_=x_sb[c][:].bitcast(F32)[:, jj * 512 : (jj + 1) * 512].rearrange("p (g r u) -> p g u r", g=2, r=P, u=2),
                )

        def transposes(c):
            xw = x_sb[c][:].bitcast(F32)
            for jj in range(JC):
                bank = tpsum.tile([P, 512], F32, name="xt")
                for b in range(4):
                    if jj in gathered(c):
                        words = gath[(c, jj)][:, b * P : (b + 1) * P]
                    else:
                        col = jj * 512 + (b // 2) * 256 + b % 2
                        words = xw[:, col : col + 255 : 2]
                    nc.tensor.transpose(bank[:, b * P : (b + 1) * P], words, ident[:])
                banks[(c, jj)] = bank

        def evacuate(c, on_dve):
            if c not in grouped:
                grouped[c] = gpool.tile([P, CH], BF16, name="grouped", align_bytes=64)
            gw = grouped[c][:].bitcast(F32)
            for jj in range(JC):
                dst = gw[:, jj * 512 : (jj + 1) * 512].rearrange("p (g r u) -> p g r u", g=2, r=P, u=2)
                src = banks[(c, jj)][:].rearrange("p (g u r) -> p g r u", g=2, u=2, r=P)
                if on_dve and jj in dve_banks(c):
                    nc.vector.tensor_copy(out=dst, in_=src)
                if not on_dve and jj not in dve_banks(c):
                    nc.scalar.copy(out=dst, in_=src)

        def quantise(c, part, parts):
            if part == 0:
                codes[c] = cpool.tile([P, CH // 4], U32, name="codes", align_bytes=64)
                scales[c] = cpool.tile([P, CH // 4], U8, name="scales", align_bytes=64)
            wd = CH // 4 // parts
            nc.vector.quantize_mx(
                out=codes[c][:, part * wd : (part + 1) * wd].bitcast(FP8X4),
                scales=scales[c][:, part * wd : (part + 1) * wd],
                in_=grouped[c][:, part * 4 * wd : (part + 1) * 4 * wd],
            )

        def multiply(c, first, count, pool, name):
            acc = pool.tile([P, 512], F32, name=name)
            accs[(c, first)] = acc
            for i in range(count):
                for g in range(2):
                    col = ((first + i) * 2 + g) * P
                    nc.tensor.matmul_mx(
                        out=acc[:, i * N : (i + 1) * N],
                        lhsT=codes[c][:, col : col + P].bitcast(FP8X4),
                        lhsT_scale=scales[c][:, col : col + P],
                        rhs=wcodes[:, g * N : (g + 1) * N].bitcast(FP8X4),
                        rhs_scale=wscales[:, g * N : (g + 1) * N],
                        start=(g == 0),
                        stop=(g == 1),
                    )

        def finish(c, first, count):
            j0 = c * JC + first
            for (a, b) in STORES:
                if a <= j0 < b:
                    if a == j0:
                        otiles[a] = opool.tile([P, (b - a) * N], F32, name="o%d" % a)
                    o_t = otiles[a]
                    off = (j0 - a) * N
                    nc.vector.tensor_tensor(
                        out=o_t[:, off : off + count * N].rearrange("p (j n) -> p j n", j=count),
                        in0=accs[(c, first)][:, 0 : count * N].rearrange("p (j n) -> p j n", j=count),
                        in1=bias[:].unsqueeze(1).to_broadcast([P, count, N]),
                        op=ALU.add,
                    )
                    if j0 + count == b:
                        nc.sync.dma_start(out=ov[:, a * N : b * N], in_=o_t[:])

        nv = const.tile([P, K], BF16, name="nv")
        ln = const.tile([P, K + N], F32, name="ln")
        sg = const.tile([P, K + N], F32, name="sg")
        th = const.tile([P, K + N], F32, name="th")
        ex = const.tile([P, K + N], F32, name="ex")
        wg = const.tile([P, K], BF16, name="wg", align_bytes=64)
        wcodes = const.tile([P, K // 4], U32, name="wcodes", align_bytes=64)
        wscales = const.tile([P, K // 4], U8, name="wscales", align_bytes=64)
        bsb = const.tile([P, 3 * N], F32, name="bsb")
        nb = const.tile([P, N], F32, name="nb")
        bias = const.tile([P, N], F32, name="bias")
        b_l = bsb[:, 0:N]
        b_s = bsb[:, N : 2 * N]
        b_e = bsb[:, 2 * N : 3 * N]

        bps = apsum.tile([P, 512], F32, name="acc")
        nc.tensor.matmul(out=bps[:, 0 : 3 * N], lhsT=ones[:], rhs=brow[:], start=True, stop=True)
        nc.vector.scalar_tensor_tensor(out=nv[:], in0=ws[:], scalar=-1.0, in1=ws[:], op0=ALU.mult, op1=ALU.min)
        nc.scalar.activation(out=ex[:, 0:K], in_=nv[:], func=ACT.Sigmoid)
        nc.scalar.activation(out=sg[:, 0:K], in_=nv[:], func=ACT.Sigmoid, bias=shift[:], scale=1.0)
        nc.vector.tensor_copy(out=bsb[:], in_=bps[:, 0 : 3 * N])
        nc.vector.scalar_tensor_tensor(out=nb[:], in0=b_s, scalar=-1.0, in1=b_s, op0=ALU.mult, op1=ALU.min)
        nc.scalar.activation(out=ex[:, K : K + N], in_=nb[:], func=ACT.Sigmoid)
        nc.scalar.activation(out=sg[:, K : K + N], in_=nb[:], func=ACT.Sigmoid, bias=shift[:], scale=1.0)
        nc.scalar.activation(out=ln[:], in_=ex[:], func=ACT.Ln, bias=one_col[:], scale=-1.0)
        nc.scalar.activation(out=th[:], in_=ln[:], func=ACT.Tanh, scale=-0.5)

        def tt(out, in0, in1, op):
            nc.vector.tensor_tensor(out=out, in0=in0, in1=in1, op=op)

        def stt(out, in0, scalar, in1, op0, op1):
            nc.vector.scalar_tensor_tensor(out=out, in0=in0, scalar=scalar, in1=in1, op0=op0, op1=op1)

        def w_relu():
            stt(ex[:, 0:K], ws[:], 0.0, ln[:, 0:K], ALU.max, ALU.subtract)

        def w_diff():
            tt(sg[:], sg[:], th[:], ALU.subtract)

        def w_softplus():
            stt(ex[:, 0:K], sg[:, 0:K], 2.0, ex[:, 0:K], ALU.mult, ALU.add)

        def w_eps():
            tt(ex[:, 0:K], ex[:, 0:K], we[:], ALU.mult)

        def w_loc_add():
            tt(
                wg[:].rearrange("p (g n t) -> p g n t", g=2, n=N, t=4),
                ex[:, 0:K].rearrange("p (g t n) -> p g n t", g=2, n=N, t=4),
                wl[:].rearrange("p (g t n) -> p g n t", g=2, n=N, t=4),
                ALU.add,
            )

        def w_quantise():
            nc.vector.quantize_mx(out=wcodes[:].bitcast(FP8X4), scales=wscales[:], in_=wg[:])

        def b_relu():
            stt(bias[:], b_s, 0.0, ln[:, K : K + N], ALU.max, ALU.subtract)

        def b_softplus():
            stt(bias[:], sg[:, K : K + N], 2.0, bias[:], ALU.mult, ALU.add)

        def b_eps():
            tt(bias[:], bias[:], b_e, ALU.mult)

        def b_loc_add():
            tt(bias[:], bias[:], b_l, ALU.add)

        LAST = NCH - 1
        made = 0
        done = 0
        for c in range(NCH):
            transposes(c)
            if c + XBUFS < NCH:
                load_x(c + XBUFS, 1)
            evacuate(c, False)
            ready = made
            while c % 2 == 1 and made <= c - (4):
                multiply(made, 0, JC, apsum, "acc")
                made += 1
            evacuate(c, True)
            while done < ready:
                finish(done, 0, JC)
                done += 1
            if c >= 1:
                quantise(c - 1, 0, 1)
            if c == 1:
                w_relu()
                w_diff()
                b_relu()
                w_softplus()
                b_softplus()
            if c == 2:
                w_eps()
                b_eps()
                w_loc_add()
                b_loc_add()
                w_quantise()
            if c >= 5 and c + 2 < NCH:
                gather(c + 2)
        while made < LAST:
            multiply(made, 0, JC, tpsum, "xt")
            made += 1
        for part in range(2):
            finish(done, 0, JC)
            done += 1
            quantise(LAST, part, 2)
        multiply(LAST, 0, 2, tpsum, "xt")
        multiply(LAST, 2, 2, tpsum, "xt")
        while done < LAST:
            finish(done, 0, JC)
            done += 1
        finish(LAST, 0, 2)
        finish(LAST, 2, 2)
